import numpy as np
import ml_dtypes


def mxq(x, axis, fmt="e4m3"):
    dtype, down = {"e4m3": (ml_dtypes.float8_e4m3fn, 7), "e5m2": (ml_dtypes.float8_e5m2, 14)}[fmt]
    v = np.moveaxis(np.asarray(x, np.float32).astype(ml_dtypes.bfloat16).astype(np.float64), axis, -1)
    blocks = v.reshape(v.shape[:-1] + (-1, 32))
    amax = np.abs(blocks).max(-1, keepdims=True)
    byte = np.maximum(np.where(amax > 0, np.frexp(amax)[1] - 1 + 127, 0) - down, 1)
    scale = np.exp2(byte - 127.0)
    codes = (blocks / scale).astype(np.float32).astype(dtype).astype(np.float64)
    return np.moveaxis((codes * scale).reshape(v.shape), -1, axis)


WIDE = False


def mx_kscale(k):
    if not WIDE:
        return np.ones(k)
    levels = np.array([10, -10, 5, -5, 0])
    a = np.random.permutation(np.resize(levels, k // 512 * 4)).reshape(k // 512, 4)
    idx = np.arange(k)
    return np.exp2(a[idx // 512, idx % 128 // 32])


BF16 = ml_dtypes.bfloat16


def bf(x):
    return np.asarray(x, np.float32).astype(BF16)


def f64(x):
    return np.asarray(x).astype(np.float64)


E2M1 = np.array([0.0, 0.5, 1.0, 1.5, 2.0, 3.0, 4.0, 6.0, -0.0, -0.5, -1.0, -1.5, -2.0, -3.0, -4.0, -6.0])


def pack_weight(w, fmt):
    k, n = w.shape
    w = f64(bf(w)).reshape(k // 32, 32, n)
    amax = np.abs(w).max(1)
    if fmt == "e4m3":
        byte = np.frexp(amax)[1] - 1 + 127 - 7
    else:
        mant, ex = np.frexp(amax / 6.0)
        byte = np.where(mant > 0.5, ex, ex - 1) + 127
    byte = np.clip(np.where(amax > 0, byte, 1), 1, 254)
    scaled = (w * np.exp2(127.0 - byte)[:, None, :]).reshape(k, n).astype(np.float32)
    by_word = np.ascontiguousarray(scaled.reshape(k // 512, 128, 4, n).transpose(0, 1, 3, 2))
    if fmt == "e4m3":
        words = by_word.astype(ml_dtypes.float8_e4m3fn).view(np.uint8)
    else:
        c = by_word.astype(ml_dtypes.float4_e2m1fn).view(np.uint8) & 0xF
        words = c[..., 0::2] | (c[..., 1::2] << 4)
    return np.ascontiguousarray(words), np.ascontiguousarray(byte.astype(np.uint8).reshape(k // 512, 16, n))


def unpack_weight(words, scales, fmt):
    g, p, n, _ = words.shape
    if fmt == "e4m3":
        vals = np.ascontiguousarray(words).view(ml_dtypes.float8_e4m3fn).astype(np.float64)
    else:
        nib = np.empty((g, p, n, 4), np.uint8)
        nib[..., 0::2] = words & 0xF
        nib[..., 1::2] = words >> 4
        vals = E2M1[nib]
    vals = vals * np.repeat(np.exp2(scales.astype(np.float64) - 127.0), 8, axis=1)[..., None]
    return vals.transpose(0, 1, 3, 2).reshape(g * 512, n)


B, E, H = 512, 1024, 1024
QH = H % 512 == 0
FMT = "e4m3"


def sigmoid(v):
    return 1.0 / (1.0 + np.exp(-v))


def setup_inputs():
    s = mx_kscale(E)
    t = mx_kscale(H) if QH else np.ones(H)
    hm = np.random.standard_normal((2, B, H))
    hm[0] = hm[0] * t

    def dw():
        return pack_weight(np.random.standard_normal((E, H)) / np.sqrt(E) / s[:, None], FMT)

    def du():
        return pack_weight(np.random.standard_normal((H, H)) / np.sqrt(H) / t[:, None], FMT)

    def db():
        return bf(np.random.standard_normal(H) * 0.1)

    out = {"x": bf(np.random.standard_normal((B, E)) * s), "hidden_memory_tm1": bf(hm)}
    for g in ("i", "f", "og", "c"):
        out["W" + g + "_words"], out["W" + g + "_scales"] = dw()
        out["U" + g + "_words"], out["U" + g + "_scales"] = du()
        out["b" + g] = db()
    return out


def reference(x, hidden_memory_tm1, Wi_words, Wi_scales, Ui_words, Ui_scales, bi, Wf_words, Wf_scales, Uf_words, Uf_scales, bf, Wog_words, Wog_scales, Uog_words, Uog_scales, bog, Wc_words, Wc_scales, Uc_words, Uc_scales, bc):
    h_prev = f64(hidden_memory_tm1)[0]
    c_prev = f64(hidden_memory_tm1)[1]
    W = np.concatenate([unpack_weight(Wi_words, Wi_scales, FMT), unpack_weight(Wf_words, Wf_scales, FMT), unpack_weight(Wog_words, Wog_scales, FMT), unpack_weight(Wc_words, Wc_scales, FMT)], axis=1)
    U = np.concatenate([unpack_weight(Ui_words, Ui_scales, FMT), unpack_weight(Uf_words, Uf_scales, FMT), unpack_weight(Uog_words, Uog_scales, FMT), unpack_weight(Uc_words, Uc_scales, FMT)], axis=1)
    b = np.concatenate([f64(bi), f64(bf), f64(bog), f64(bc)], axis=0)
    gx = mxq(f64(x), 1, "e4m3") @ W
    if QH:
        gh = mxq(h_prev, 1, "e4m3") @ U
    else:
        gh = h_prev @ U
    gates = gx + gh + b
    i = sigmoid(gates[:, 0 * H:1 * H])
    f = sigmoid(gates[:, 1 * H:2 * H])
    o = sigmoid(gates[:, 2 * H:3 * H])
    c_ = np.tanh(gates[:, 3 * H:4 * H])
    c = f * c_prev + i * c_
    h = o * np.tanh(c)
    return np.stack([h, c])

@@ -1,0 +1,181 @@
+from contextlib import ExitStack
+
+import concourse.mybir as mybir
+from concourse.masks import make_identity
+
+F32 = mybir.dt.float32
+BF16 = mybir.dt.bfloat16
+I32 = mybir.dt.int32
+U32 = mybir.dt.uint32
+U8 = mybir.dt.uint8
+FP8X4 = mybir.dt.float8_e4m3fn_x4
+ACT = mybir.ActivationFunctionType
+ALU = mybir.AluOpType
+
+P = 128
+BATCH, E, H = 512, 1024, 1024
+PACK = 4
+K_PASS = P * PACK
+K_GROUPS = E // K_PASS
+BANK = 512
+BATCH_TILES = BATCH // P
+HALVES = H // BANK
+SOURCES = 2
+QUADRANTS = 4
+SCALE_ROWS = 4
+
+FLOPS = 2 * BATCH * (E + H) * 4 * H
+
+
+def tile_create_recurrent_unit_kernel(
+    tc,
+    x, hidden_memory_tm1,
+    Wi_words, Wi_scales, Ui_words, Ui_scales, bi,
+    Wf_words, Wf_scales, Uf_words, Uf_scales, bf,
+    Wog_words, Wog_scales, Uog_words, Uog_scales, bog,
+    Wc_words, Wc_scales, Uc_words, Uc_scales, bc,
+    out,
+):
+    nc = tc.nc
+    h_prev = hidden_memory_tm1[0]
+    c_prev = hidden_memory_tm1[1]
+
+    gate_names = ["f", "i", "c_", "o"]
+    gate_words = {"i": (Wi_words, Ui_words), "c_": (Wc_words, Uc_words),
+                  "f": (Wf_words, Uf_words), "o": (Wog_words, Uog_words)}
+    gate_scales = {"i": (Wi_scales, Ui_scales), "c_": (Wc_scales, Uc_scales),
+                   "f": (Wf_scales, Uf_scales), "o": (Wog_scales, Uog_scales)}
+    gate_bias = {"i": bi, "c_": bc, "f": bf, "o": bog}
+    gate_func = {"i": ACT.Sigmoid, "c_": ACT.Tanh, "f": ACT.Sigmoid, "o": ACT.Sigmoid}
+
+    with ExitStack() as ctx:
+        keep = ctx.enter_context(tc.tile_pool(name="keep", bufs=1))
+        psum = ctx.enter_context(tc.psum_pool(name="psum", bufs=8))
+
+        planes = {}
+        for name in gate_names:
+            planes[name] = keep.tile([P, H], U8, align_bytes=64, name="planes_" + name)
+            nc.vector.memset(planes[name][:].bitcast(I32), 0)
+        bias_rows = keep.tile([P, len(gate_names), H], BF16, name="bias_rows")
+        nc.vector.memset(bias_rows[:].rearrange("p j n -> p (j n)").bitcast(I32), 0)
+        ones = keep.tile([P, P], BF16, name="ones")
+        nc.vector.memset(ones[:], 1.0)
+        identity = keep.tile([P, P], F32, name="identity")
+        make_identity(nc, identity[:])
+
+        for j, name in enumerate(gate_names):
+            nc.scalar.dma_start(out=bias_rows[0:1, j, :], in_=gate_bias[name].unsqueeze(0))
+
+        rows = {}
+        for s, source in enumerate((x, h_prev)):
+            for m in range(BATCH_TILES):
+                rows[s, m] = keep.tile([P, E], BF16, name="rows_%d_%d" % (s, m))
+                nc.sync.dma_start(out=rows[s, m][:], in_=source[m * P:(m + 1) * P, :])
+
+        words = {}
+        c_old = {}
+        for name in gate_names:
+            for s in range(SOURCES):
+                for quadrant in range(QUADRANTS):
+                    first = 32 * quadrant + SCALE_ROWS * K_GROUPS * s
+                    nc.sync.dma_start(
+                        out=planes[name][first:first + SCALE_ROWS * K_GROUPS, :].bitcast(I32),
+                        in_=gate_scales[name][s][
+                            :, SCALE_ROWS * quadrant:SCALE_ROWS * (quadrant + 1), :].bitcast(I32),
+                    )
+            for half in range(HALVES):
+                for s in range(SOURCES):
+                    for g in range(K_GROUPS):
+                        words[name, half, s, g] = keep.tile(
+                            [P, BANK * PACK], U8, align_bytes=64,
+                            name="words_%s_%d_%d_%d" % (name, half, s, g))
+                        nc.sync.dma_start(
+                            out=words[name, half, s, g][:].bitcast(I32),
+                            in_=gate_words[name][s][g].rearrange("p n t -> p (n t)")[
+                                :, half * BANK * PACK:(half + 1) * BANK * PACK].bitcast(I32),
+                        )
+            if name == "f":
+                for m in range(BATCH_TILES):
+                    c_old[m] = keep.tile([P, H], BF16, name="c_old_%d" % m)
+                    nc.sync.dma_start(out=c_old[m][:], in_=c_prev[m * P:(m + 1) * P, :])
+
+        codes = {}
+        code_scales = {}
+
+        def quantise_rows(s, m):
+            pairs = rows[s, m][:].bitcast(F32)
+            turned = psum.tile([P, K_GROUPS, 2, P], F32, tag="bank", name="turned_%d_%d" % (s, m))
+            for g in range(K_GROUPS):
+                for u in range(2):
+                    nc.tensor.transpose(
+                        turned[:, g, u, :],
+                        pairs[:, (K_PASS // 2) * g + u:(K_PASS // 2) * (g + 1):2],
+                        identity[:],
+                    )
+            grouped = keep.tile([P, K_GROUPS * P * PACK], BF16, align_bytes=64,
+                                name="grouped_%d_%d" % (s, m))
+            nc.scalar.copy(
+                out=grouped[:].bitcast(F32).rearrange("p (g r u) -> p g r u", g=K_GROUPS, u=2),
+                in_=turned[:].rearrange("p g u r -> p g r u"),
+            )
+            codes[s, m] = keep.tile([P, K_GROUPS * P], U32, align_bytes=64, name="codes_%d_%d" % (s, m))
+            code_scales[s, m] = keep.tile([P, K_GROUPS * P], U8, align_bytes=64,
+                                          name="code_scales_%d_%d" % (s, m))
+            nc.vector.quantize_mx(out=codes[s, m][:].bitcast(FP8X4), scales=code_scales[s, m][:],
+                                  in_=grouped[:])
+
+        for m in range(BATCH_TILES):
+            quantise_rows(0, m)
+
+        bias_all = {}
+        for j, name in enumerate(gate_names):
+            spread = psum.tile([P, H], BF16, tag="bank", name="spread_" + name)
+            for half in range(HALVES):
+                nc.tensor.matmul(out=spread[:, half * BANK:(half + 1) * BANK], lhsT=ones[:],
+                                 rhs=bias_rows[:, j, half * BANK:(half + 1) * BANK],
+                                 start=True, stop=True)
+            bias_all[name] = keep.tile([P, H], BF16, name="bias_all_" + name)
+            nc.vector.tensor_copy(out=bias_all[name][:], in_=spread[:])
+
+        for m in range(BATCH_TILES):
+            quantise_rows(1, m)
+
+        gate = {}
+        for name in gate_names:
+            for half in range(HALVES):
+                cols = slice(half * BANK, (half + 1) * BANK)
+                for m in range(BATCH_TILES):
+                    batch = slice(m * P, (m + 1) * P)
+                    acc = psum.tile([P, BANK], F32, tag="bank", name="acc_%s_%d_%d" % (name, half, m))
+                    for s in range(SOURCES):
+                        for g in range(K_GROUPS):
+                            first = SCALE_ROWS * (K_GROUPS * s + g)
+                            nc.tensor.matmul_mx(
+                                out=acc[:],
+                                lhsT=codes[s, m][:, g * P:(g + 1) * P].bitcast(FP8X4),
+                                lhsT_scale=code_scales[s, m][:, g * P:(g + 1) * P],
+                                rhs=words[name, half, s, g][:].bitcast(FP8X4),
+                                rhs_scale=planes[name][first:P, cols],
+                                start=(s == 0 and g == 0),
+                                stop=(s == SOURCES - 1 and g == K_GROUPS - 1),
+                            )
+                    here = keep.tile([P, BANK], F32, name="gate_%s_%d_%d" % (name, half, m))
+                    gate[name, half, m] = here
+                    nc.vector.tensor_tensor(out=here[:], in0=acc[:], in1=bias_all[name][:, cols],
+                                            op=ALU.add)
+                    nc.scalar.activation(out=here[:], in_=here[:], func=gate_func[name])
+
+                    if name == "f":
+                        nc.vector.tensor_tensor(out=here[:], in0=here[:], in1=c_old[m][:, cols],
+                                                op=ALU.mult)
+                    if name == "c_":
+                        nc.gpsimd.tensor_tensor(out=here[:], in0=here[:], in1=gate["i", half, m][:],
+                                                op=ALU.mult)
+                        nc.vector.tensor_tensor(out=here[:], in0=here[:], in1=gate["f", half, m][:],
+                                                op=ALU.add)
+                        nc.sync.dma_start(out=out[1, batch, cols], in_=here[:])
+                        nc.scalar.activation(out=gate["i", half, m][:], in_=here[:], func=ACT.Tanh)
+                    if name == "o":
+                        nc.vector.tensor_tensor(out=here[:], in0=here[:], in1=gate["i", half, m][:],
+                                                op=ALU.mult)
+                        nc.sync.dma_start(out=out[0, batch, cols], in_=here[:])

@@ -23,6 +23,8 @@ HALVES = H // BANK
 SOURCES = 2
 QUADRANTS = 4
 SCALE_ROWS = 4
+PRODUCT_LAG = 1
+CELL_LAG = 5
 
 FLOPS = 2 * BATCH * (E + H) * 4 * H
 
@@ -51,6 +53,7 @@ def tile_create_recurrent_unit_kernel(
     with ExitStack() as ctx:
         keep = ctx.enter_context(tc.tile_pool(name="keep", bufs=1))
         psum = ctx.enter_context(tc.psum_pool(name="psum", bufs=8))
+        ctx.enter_context(tc.manual_schedule())
 
         planes = {}
         for name in gate_names:
@@ -77,9 +80,9 @@ def tile_create_recurrent_unit_kernel(
         for name in gate_names:
             for s in range(SOURCES):
                 for quadrant in range(QUADRANTS):
-                    first = 32 * quadrant + SCALE_ROWS * K_GROUPS * s
+                    top = 32 * quadrant + SCALE_ROWS * K_GROUPS * s
                     nc.sync.dma_start(
-                        out=planes[name][first:first + SCALE_ROWS * K_GROUPS, :].bitcast(I32),
+                        out=planes[name][top:top + SCALE_ROWS * K_GROUPS, :].bitcast(I32),
                         in_=gate_scales[name][s][
                             :, SCALE_ROWS * quadrant:SCALE_ROWS * (quadrant + 1), :].bitcast(I32),
                     )
@@ -141,41 +144,53 @@ def tile_create_recurrent_unit_kernel(
             quantise_rows(1, m)
 
         gate = {}
-        for name in gate_names:
-            for half in range(HALVES):
-                cols = slice(half * BANK, (half + 1) * BANK)
-                for m in range(BATCH_TILES):
-                    batch = slice(m * P, (m + 1) * P)
-                    acc = psum.tile([P, BANK], F32, tag="bank", name="acc_%s_%d_%d" % (name, half, m))
-                    for s in range(SOURCES):
-                        for g in range(K_GROUPS):
-                            first = SCALE_ROWS * (K_GROUPS * s + g)
-                            nc.tensor.matmul_mx(
-                                out=acc[:],
-                                lhsT=codes[s, m][:, g * P:(g + 1) * P].bitcast(FP8X4),
-                                lhsT_scale=code_scales[s, m][:, g * P:(g + 1) * P],
-                                rhs=words[name, half, s, g][:].bitcast(FP8X4),
-                                rhs_scale=planes[name][first:P, cols],
-                                start=(s == 0 and g == 0),
-                                stop=(s == SOURCES - 1 and g == K_GROUPS - 1),
-                            )
-                    here = keep.tile([P, BANK], F32, name="gate_%s_%d_%d" % (name, half, m))
-                    gate[name, half, m] = here
-                    nc.vector.tensor_tensor(out=here[:], in0=acc[:], in1=bias_all[name][:, cols],
-                                            op=ALU.add)
-                    nc.scalar.activation(out=here[:], in_=here[:], func=gate_func[name])
 
-                    if name == "f":
-                        nc.vector.tensor_tensor(out=here[:], in0=here[:], in1=c_old[m][:, cols],
-                                                op=ALU.mult)
-                    if name == "c_":
-                        nc.gpsimd.tensor_tensor(out=here[:], in0=here[:], in1=gate["i", half, m][:],
-                                                op=ALU.mult)
-                        nc.vector.tensor_tensor(out=here[:], in0=here[:], in1=gate["f", half, m][:],
-                                                op=ALU.add)
-                        nc.sync.dma_start(out=out[1, batch, cols], in_=here[:])
-                        nc.scalar.activation(out=gate["i", half, m][:], in_=here[:], func=ACT.Tanh)
-                    if name == "o":
-                        nc.vector.tensor_tensor(out=here[:], in0=here[:], in1=gate["i", half, m][:],
-                                                op=ALU.mult)
-                        nc.sync.dma_start(out=out[0, batch, cols], in_=here[:])
+        def gate_values(name, half, m):
+            cols = slice(half * BANK, (half + 1) * BANK)
+            acc = psum.tile([P, BANK], F32, tag="bank", name="acc_%s_%d_%d" % (name, half, m))
+            for s in range(SOURCES):
+                for g in range(K_GROUPS):
+                    top = SCALE_ROWS * (K_GROUPS * s + g)
+                    nc.tensor.matmul_mx(
+                        out=acc[:],
+                        lhsT=codes[s, m][:, g * P:(g + 1) * P].bitcast(FP8X4),
+                        lhsT_scale=code_scales[s, m][:, g * P:(g + 1) * P],
+                        rhs=words[name, half, s, g][:].bitcast(FP8X4),
+                        rhs_scale=planes[name][top:P, cols],
+                        start=(s == 0 and g == 0),
+                        stop=(s == SOURCES - 1 and g == K_GROUPS - 1),
+                    )
+            gate[name, half, m] = keep.tile([P, BANK], F32, name="gate_%s_%d_%d" % (name, half, m))
+            nc.vector.tensor_tensor(out=gate[name, half, m][:], in0=acc[:],
+                                    in1=bias_all[name][:, cols], op=ALU.add)
+            nc.scalar.activation(out=gate[name, half, m][:], in_=gate[name, half, m][:],
+                                 func=gate_func[name])
+
+        def product(name, half, m):
+            cols = slice(half * BANK, (half + 1) * BANK)
+            here = gate[name, half, m]
+            if name == "f":
+                nc.gpsimd.tensor_tensor(out=here[:], in0=here[:], in1=c_old[m][:, cols], op=ALU.mult)
+            if name == "c_":
+                nc.gpsimd.tensor_tensor(out=here[:], in0=here[:], in1=gate["i", half, m][:], op=ALU.mult)
+            if name == "o":
+                nc.vector.tensor_tensor(out=here[:], in0=here[:], in1=gate["i", half, m][:], op=ALU.mult)
+                nc.sync.dma_start(out=out[0, m * P:(m + 1) * P, cols], in_=here[:])
+
+        def cell_state(name, half, m):
+            cols = slice(half * BANK, (half + 1) * BANK)
+            if name == "c_":
+                here = gate[name, half, m]
+                nc.vector.tensor_tensor(out=here[:], in0=here[:], in1=gate["f", half, m][:], op=ALU.add)
+                nc.sync.dma_start(out=out[1, m * P:(m + 1) * P, cols], in_=here[:])
+                nc.scalar.activation(out=gate["i", half, m][:], in_=here[:], func=ACT.Tanh)
+
+        banks = [(name, half, m) for name in gate_names for half in range(HALVES)
+                 for m in range(BATCH_TILES)]
+        for n in range(len(banks) + CELL_LAG):
+            if n < len(banks):
+                gate_values(*banks[n])
+            if 0 <= n - PRODUCT_LAG < len(banks):
+                product(*banks[n - PRODUCT_LAG])
+            if 0 <= n - CELL_LAG < len(banks):
+                cell_state(*banks[n - CELL_LAG])

@@ -23,8 +23,9 @@ HALVES = H // BANK
 SOURCES = 2
 QUADRANTS = 4
 SCALE_ROWS = 4
+PAIR = 2
 PRODUCT_LAG = 1
-CELL_LAG = 5
+CELL_LAG = 4
 
 FLOPS = 2 * BATCH * (E + H) * 4 * H
 
@@ -55,29 +56,32 @@ def tile_create_recurrent_unit_kernel(
         psum = ctx.enter_context(tc.psum_pool(name="psum", bufs=8))
         ctx.enter_context(tc.manual_schedule())
 
+        bias_row = {}
+        for name in gate_names:
+            bias_row[name] = keep.tile([P, H], BF16, name="bias_row_" + name)
+            nc.vector.memset(bias_row[name][:].bitcast(I32), 0)
+            nc.scalar.dma_start(out=bias_row[name][0:1, :], in_=gate_bias[name].unsqueeze(0))
+        ones = keep.tile([P, P], BF16, name="ones")
+        nc.vector.memset(ones[:], 1.0)
         planes = {}
         for name in gate_names:
             planes[name] = keep.tile([P, H], U8, align_bytes=64, name="planes_" + name)
             nc.vector.memset(planes[name][:].bitcast(I32), 0)
-        bias_rows = keep.tile([P, len(gate_names), H], BF16, name="bias_rows")
-        nc.vector.memset(bias_rows[:].rearrange("p j n -> p (j n)").bitcast(I32), 0)
-        ones = keep.tile([P, P], BF16, name="ones")
-        nc.vector.memset(ones[:], 1.0)
         identity = keep.tile([P, P], F32, name="identity")
         make_identity(nc, identity[:])
 
-        for j, name in enumerate(gate_names):
-            nc.scalar.dma_start(out=bias_rows[0:1, j, :], in_=gate_bias[name].unsqueeze(0))
+        def load_rows(source, label):
+            tiles = []
+            for pair in range(BATCH_TILES // PAIR):
+                tiles.append(keep.tile([P, PAIR, E], BF16, name="%s_%d" % (label, pair)))
+                nc.sync.dma_start(
+                    out=tiles[pair][:],
+                    in_=source[pair * PAIR * P:(pair + 1) * PAIR * P, :].rearrange(
+                        "(t p) k -> p t k", p=P),
+                )
+            return tiles
 
-        rows = {}
-        for s, source in enumerate((x, h_prev)):
-            for m in range(BATCH_TILES):
-                rows[s, m] = keep.tile([P, E], BF16, name="rows_%d_%d" % (s, m))
-                nc.sync.dma_start(out=rows[s, m][:], in_=source[m * P:(m + 1) * P, :])
-
-        words = {}
-        c_old = {}
-        for name in gate_names:
+        def load_scales(name):
             for s in range(SOURCES):
                 for quadrant in range(QUADRANTS):
                     top = 32 * quadrant + SCALE_ROWS * K_GROUPS * s
@@ -86,6 +90,10 @@ def tile_create_recurrent_unit_kernel(
                         in_=gate_scales[name][s][
                             :, SCALE_ROWS * quadrant:SCALE_ROWS * (quadrant + 1), :].bitcast(I32),
                     )
+
+        words = {}
+
+        def load_words(name):
             for half in range(HALVES):
                 for s in range(SOURCES):
                     for g in range(K_GROUPS):
@@ -97,16 +105,34 @@ def tile_create_recurrent_unit_kernel(
                             in_=gate_words[name][s][g].rearrange("p n t -> p (n t)")[
                                 :, half * BANK * PACK:(half + 1) * BANK * PACK].bitcast(I32),
                         )
-            if name == "f":
-                for m in range(BATCH_TILES):
-                    c_old[m] = keep.tile([P, H], BF16, name="c_old_%d" % m)
-                    nc.sync.dma_start(out=c_old[m][:], in_=c_prev[m * P:(m + 1) * P, :])
+
+        x_rows = load_rows(x, "x_rows")
+        load_scales("f")
+        h_rows = load_rows(h_prev, "h_rows")
+        load_words("f")
+        c_old = load_rows(c_prev, "c_old")
+        for name in gate_names[1:]:
+            load_scales(name)
+            load_words(name)
+
+        spread = {}
+        bias_all = {}
+
+        def spread_bias(name, half):
+            if half == 0:
+                spread[name] = psum.tile([P, H], BF16, tag="bank", name="spread_" + name)
+            cols = slice(half * BANK, (half + 1) * BANK)
+            nc.tensor.matmul(out=spread[name][:, cols], lhsT=ones[:], rhs=bias_row[name][:, cols],
+                             start=True, stop=True)
+            if half == HALVES - 1:
+                bias_all[name] = keep.tile([P, H], BF16, name="bias_all_" + name)
+                nc.vector.tensor_copy(out=bias_all[name][:], in_=spread[name][:])
 
         codes = {}
         code_scales = {}
 
-        def quantise_rows(s, m):
-            pairs = rows[s, m][:].bitcast(F32)
+        def quantise_rows(s, m, bf16_rows):
+            pairs = bf16_rows.bitcast(F32)
             turned = psum.tile([P, K_GROUPS, 2, P], F32, tag="bank", name="turned_%d_%d" % (s, m))
             for g in range(K_GROUPS):
                 for u in range(2):
@@ -127,21 +153,14 @@ def tile_create_recurrent_unit_kernel(
             nc.vector.quantize_mx(out=codes[s, m][:].bitcast(FP8X4), scales=code_scales[s, m][:],
                                   in_=grouped[:])
 
-        for m in range(BATCH_TILES):
-            quantise_rows(0, m)
-
-        bias_all = {}
-        for j, name in enumerate(gate_names):
-            spread = psum.tile([P, H], BF16, tag="bank", name="spread_" + name)
+        for name in gate_names[:2]:
             for half in range(HALVES):
-                nc.tensor.matmul(out=spread[:, half * BANK:(half + 1) * BANK], lhsT=ones[:],
-                                 rhs=bias_rows[:, j, half * BANK:(half + 1) * BANK],
-                                 start=True, stop=True)
-            bias_all[name] = keep.tile([P, H], BF16, name="bias_all_" + name)
-            nc.vector.tensor_copy(out=bias_all[name][:], in_=spread[:])
-
-        for m in range(BATCH_TILES):
-            quantise_rows(1, m)
+                spread_bias(name, half)
+        for s, tiles in enumerate((x_rows, h_rows)):
+            for pair in range(BATCH_TILES // PAIR):
+                for t in range(PAIR):
+                    quantise_rows(s, pair * PAIR + t, tiles[pair][:, t, :])
+                spread_bias(gate_names[2 + s], pair)
 
         gate = {}
 
@@ -170,11 +189,13 @@ def tile_create_recurrent_unit_kernel(
             cols = slice(half * BANK, (half + 1) * BANK)
             here = gate[name, half, m]
             if name == "f":
-                nc.gpsimd.tensor_tensor(out=here[:], in0=here[:], in1=c_old[m][:, cols], op=ALU.mult)
+                nc.gpsimd.tensor_tensor(out=here[:], in0=here[:],
+                                        in1=c_old[m // PAIR][:, m % PAIR, cols], op=ALU.mult)
             if name == "c_":
                 nc.gpsimd.tensor_tensor(out=here[:], in0=here[:], in1=gate["i", half, m][:], op=ALU.mult)
             if name == "o":
-                nc.vector.tensor_tensor(out=here[:], in0=here[:], in1=gate["i", half, m][:], op=ALU.mult)
+                engine = nc.vector if half == HALVES - 1 else nc.gpsimd
+                engine.tensor_tensor(out=here[:], in0=here[:], in1=gate["i", half, m][:], op=ALU.mult)
                 nc.sync.dma_start(out=out[0, m * P:(m + 1) * P, cols], in_=here[:])
 
         def cell_state(name, half, m):
@@ -190,7 +211,7 @@ def tile_create_recurrent_unit_kernel(
         for n in range(len(banks) + CELL_LAG):
             if n < len(banks):
                 gate_values(*banks[n])
-            if 0 <= n - PRODUCT_LAG < len(banks):
-                product(*banks[n - PRODUCT_LAG])
             if 0 <= n - CELL_LAG < len(banks):
                 cell_state(*banks[n - CELL_LAG])
+            if 0 <= n - PRODUCT_LAG < len(banks):
+                product(*banks[n - PRODUCT_LAG])

@@ -23,7 +23,7 @@ HALVES = H // BANK
 SOURCES = 2
 QUADRANTS = 4
 SCALE_ROWS = 4
-PAIR = 2
+WARM_UP = 4
 PRODUCT_LAG = 1
 CELL_LAG = 4
 
@@ -56,40 +56,37 @@ def tile_create_recurrent_unit_kernel(
         psum = ctx.enter_context(tc.psum_pool(name="psum", bufs=8))
         ctx.enter_context(tc.manual_schedule())
 
+        planes = {}
+        for name in gate_names:
+            planes[name] = keep.tile([P, H], U8, align_bytes=64, name="planes_" + name)
+        nc.vector.memset(planes[gate_names[0]][:].bitcast(I32), 0)
+        ones = keep.tile([P, BANK], BF16, name="ones")
+        nc.vector.memset(ones[:], 1.0)
+        identity = keep.tile([P, P], F32, name="identity")
+        make_identity(nc, identity[:])
         bias_row = {}
         for name in gate_names:
             bias_row[name] = keep.tile([P, H], BF16, name="bias_row_" + name)
             nc.vector.memset(bias_row[name][:].bitcast(I32), 0)
-            nc.scalar.dma_start(out=bias_row[name][0:1, :], in_=gate_bias[name].unsqueeze(0))
-        ones = keep.tile([P, P], BF16, name="ones")
-        nc.vector.memset(ones[:], 1.0)
-        planes = {}
-        for name in gate_names:
-            planes[name] = keep.tile([P, H], U8, align_bytes=64, name="planes_" + name)
+            nc.gpsimd.dma_start(out=bias_row[name][0:1, :], in_=gate_bias[name].unsqueeze(0))
+        for name in gate_names[1:]:
             nc.vector.memset(planes[name][:].bitcast(I32), 0)
-        identity = keep.tile([P, P], F32, name="identity")
-        make_identity(nc, identity[:])
 
         def load_rows(source, label):
             tiles = []
-            for pair in range(BATCH_TILES // PAIR):
-                tiles.append(keep.tile([P, PAIR, E], BF16, name="%s_%d" % (label, pair)))
-                nc.sync.dma_start(
-                    out=tiles[pair][:],
-                    in_=source[pair * PAIR * P:(pair + 1) * PAIR * P, :].rearrange(
-                        "(t p) k -> p t k", p=P),
-                )
+            for m in range(BATCH_TILES):
+                tiles.append(keep.tile([P, E], BF16, name="%s_%d" % (label, m)))
+                nc.sync.dma_start(out=tiles[m][:], in_=source[m * P:(m + 1) * P, :])
             return tiles
 
-        def load_scales(name):
-            for s in range(SOURCES):
-                for quadrant in range(QUADRANTS):
-                    top = 32 * quadrant + SCALE_ROWS * K_GROUPS * s
-                    nc.sync.dma_start(
-                        out=planes[name][top:top + SCALE_ROWS * K_GROUPS, :].bitcast(I32),
-                        in_=gate_scales[name][s][
-                            :, SCALE_ROWS * quadrant:SCALE_ROWS * (quadrant + 1), :].bitcast(I32),
-                    )
+        def load_scales(name, s):
+            for quadrant in range(QUADRANTS):
+                top = 32 * quadrant + SCALE_ROWS * K_GROUPS * s
+                nc.sync.dma_start(
+                    out=planes[name][top:top + SCALE_ROWS * K_GROUPS, :].bitcast(I32),
+                    in_=gate_scales[name][s][
+                        :, SCALE_ROWS * quadrant:SCALE_ROWS * (quadrant + 1), :].bitcast(I32),
+                )
 
         words = {}
 
@@ -107,26 +104,26 @@ def tile_create_recurrent_unit_kernel(
                         )
 
         x_rows = load_rows(x, "x_rows")
-        load_scales("f")
+        load_scales("f", 0)
         h_rows = load_rows(h_prev, "h_rows")
+        load_scales("f", 1)
         load_words("f")
         c_old = load_rows(c_prev, "c_old")
         for name in gate_names[1:]:
-            load_scales(name)
+            for s in range(SOURCES):
+                load_scales(name, s)
             load_words(name)
 
-        spread = {}
         bias_all = {}
 
-        def spread_bias(name, half):
-            if half == 0:
-                spread[name] = psum.tile([P, H], BF16, tag="bank", name="spread_" + name)
-            cols = slice(half * BANK, (half + 1) * BANK)
-            nc.tensor.matmul(out=spread[name][:, cols], lhsT=ones[:], rhs=bias_row[name][:, cols],
-                             start=True, stop=True)
-            if half == HALVES - 1:
-                bias_all[name] = keep.tile([P, H], BF16, name="bias_all_" + name)
-                nc.vector.tensor_copy(out=bias_all[name][:], in_=spread[name][:])
+        def spread_bias(name):
+            spread = psum.tile([P, H], BF16, tag="bank", name="spread_" + name)
+            for half in range(HALVES):
+                cols = slice(half * BANK, (half + 1) * BANK)
+                nc.tensor.matmul(out=spread[:, cols], lhsT=ones[:, :P], rhs=bias_row[name][:, cols],
+                                 start=True, stop=True)
+            bias_all[name] = keep.tile([P, H], BF16, name="bias_all_" + name)
+            nc.vector.tensor_copy(out=bias_all[name][:], in_=spread[:])
 
         codes = {}
         code_scales = {}
@@ -153,14 +150,14 @@ def tile_create_recurrent_unit_kernel(
             nc.vector.quantize_mx(out=codes[s, m][:].bitcast(FP8X4), scales=code_scales[s, m][:],
                                   in_=grouped[:])
 
-        for name in gate_names[:2]:
-            for half in range(HALVES):
-                spread_bias(name, half)
-        for s, tiles in enumerate((x_rows, h_rows)):
-            for pair in range(BATCH_TILES // PAIR):
-                for t in range(PAIR):
-                    quantise_rows(s, pair * PAIR + t, tiles[pair][:, t, :])
-                spread_bias(gate_names[2 + s], pair)
+        unread = psum.tile([P, BANK], F32, tag="bank", name="unread")
+        for repeat in range(WARM_UP):
+            nc.tensor.matmul(out=unread[:], lhsT=ones[:, :P], rhs=ones[:], start=True, stop=True)
+        for m in range(BATCH_TILES):
+            quantise_rows(0, m, x_rows[m][:])
+        for m in range(BATCH_TILES):
+            quantise_rows(1, m, h_rows[m][:])
+            spread_bias(gate_names[m])
 
         gate = {}
 
@@ -189,8 +186,7 @@ def tile_create_recurrent_unit_kernel(
             cols = slice(half * BANK, (half + 1) * BANK)
             here = gate[name, half, m]
             if name == "f":
-                nc.gpsimd.tensor_tensor(out=here[:], in0=here[:],
-                                        in1=c_old[m // PAIR][:, m % PAIR, cols], op=ALU.mult)
+                nc.gpsimd.tensor_tensor(out=here[:], in0=here[:], in1=c_old[m][:, cols], op=ALU.mult)
             if name == "c_":
                 nc.gpsimd.tensor_tensor(out=here[:], in0=here[:], in1=gate["i", half, m][:], op=ALU.mult)
             if name == "o":

@@ -24,8 +24,20 @@ SOURCES = 2
 QUADRANTS = 4
 SCALE_ROWS = 4
 WARM_UP = 4
-PRODUCT_LAG = 1
-CELL_LAG = 4
+LAG_PRODUCT = 1
+LAG_CELL = 1
+LAG_HIDDEN = 1
+C_OLD_AFTER = "i"
+
+
+def ON_GPSIMD(op, half, m):
+    return op == "fc"
+
+
+def BANKS(gate_names):
+    return ([(name, 0, m) for name in gate_names for m in range(BATCH_TILES)]
+            + [(name, 1, 2 * pair + e) for pair in range(2) for name in gate_names for e in range(2)])
+
 
 FLOPS = 2 * BATCH * (E + H) * 4 * H
 
@@ -90,29 +102,31 @@ def tile_create_recurrent_unit_kernel(
 
         words = {}
 
-        def load_words(name):
-            for half in range(HALVES):
-                for s in range(SOURCES):
-                    for g in range(K_GROUPS):
-                        words[name, half, s, g] = keep.tile(
-                            [P, BANK * PACK], U8, align_bytes=64,
-                            name="words_%s_%d_%d_%d" % (name, half, s, g))
-                        nc.sync.dma_start(
-                            out=words[name, half, s, g][:].bitcast(I32),
-                            in_=gate_words[name][s][g].rearrange("p n t -> p (n t)")[
-                                :, half * BANK * PACK:(half + 1) * BANK * PACK].bitcast(I32),
-                        )
+        def load_words(name, half, s):
+            words[name, half, s] = keep.tile([P, K_GROUPS * BANK * PACK], U8, align_bytes=64,
+                                             name="words_%s_%d_%d" % (name, half, s))
+            nc.sync.dma_start(
+                out=words[name, half, s][:].bitcast(I32).rearrange("p (g w) -> p g w", g=K_GROUPS),
+                in_=gate_words[name][s].rearrange("g p n t -> p g (n t)")[
+                    :, :, half * BANK * PACK:(half + 1) * BANK * PACK].bitcast(I32),
+            )
 
         x_rows = load_rows(x, "x_rows")
         load_scales("f", 0)
         h_rows = load_rows(h_prev, "h_rows")
         load_scales("f", 1)
-        load_words("f")
-        c_old = load_rows(c_prev, "c_old")
+        for s in range(SOURCES):
+            load_words("f", 0, s)
+        c_old = None
         for name in gate_names[1:]:
             for s in range(SOURCES):
                 load_scales(name, s)
-            load_words(name)
+                load_words(name, 0, s)
+            if name == C_OLD_AFTER:
+                c_old = load_rows(c_prev, "c_old")
+        for name in gate_names:
+            for s in range(SOURCES):
+                load_words(name, 1, s)
 
         bias_all = {}
 
@@ -171,7 +185,7 @@ def tile_create_recurrent_unit_kernel(
                         out=acc[:],
                         lhsT=codes[s, m][:, g * P:(g + 1) * P].bitcast(FP8X4),
                         lhsT_scale=code_scales[s, m][:, g * P:(g + 1) * P],
-                        rhs=words[name, half, s, g][:].bitcast(FP8X4),
+                        rhs=words[name, half, s][:, g * BANK * PACK:(g + 1) * BANK * PACK].bitcast(FP8X4),
                         rhs_scale=planes[name][top:P, cols],
                         start=(s == 0 and g == 0),
                         stop=(s == SOURCES - 1 and g == K_GROUPS - 1),
@@ -182,32 +196,52 @@ def tile_create_recurrent_unit_kernel(
             nc.scalar.activation(out=gate[name, half, m][:], in_=gate[name, half, m][:],
                                  func=gate_func[name])
 
-        def product(name, half, m):
-            cols = slice(half * BANK, (half + 1) * BANK)
-            here = gate[name, half, m]
-            if name == "f":
-                nc.gpsimd.tensor_tensor(out=here[:], in0=here[:], in1=c_old[m][:, cols], op=ALU.mult)
-            if name == "c_":
-                nc.gpsimd.tensor_tensor(out=here[:], in0=here[:], in1=gate["i", half, m][:], op=ALU.mult)
-            if name == "o":
-                engine = nc.vector if half == HALVES - 1 else nc.gpsimd
-                engine.tensor_tensor(out=here[:], in0=here[:], in1=gate["i", half, m][:], op=ALU.mult)
-                nc.sync.dma_start(out=out[0, m * P:(m + 1) * P, cols], in_=here[:])
+        def engine_of(op, half, m):
+            return nc.gpsimd if ON_GPSIMD(op, half, m) else nc.vector
 
-        def cell_state(name, half, m):
+        def forget(half, m):
             cols = slice(half * BANK, (half + 1) * BANK)
-            if name == "c_":
-                here = gate[name, half, m]
-                nc.vector.tensor_tensor(out=here[:], in0=here[:], in1=gate["f", half, m][:], op=ALU.add)
-                nc.sync.dma_start(out=out[1, m * P:(m + 1) * P, cols], in_=here[:])
-                nc.scalar.activation(out=gate["i", half, m][:], in_=here[:], func=ACT.Tanh)
+            here = gate["f", half, m]
+            engine_of("fc", half, m).tensor_tensor(out=here[:], in0=here[:], in1=c_old[m][:, cols], op=ALU.mult)
 
-        banks = [(name, half, m) for name in gate_names for half in range(HALVES)
-                 for m in range(BATCH_TILES)]
-        for n in range(len(banks) + CELL_LAG):
+        def remember(half, m):
+            here = gate["c_", half, m]
+            engine_of("ic", half, m).tensor_tensor(out=here[:], in0=here[:], in1=gate["i", half, m][:], op=ALU.mult)
+
+        def cell_state(half, m):
+            cols = slice(half * BANK, (half + 1) * BANK)
+            here = gate["c_", half, m]
+            engine_of("cadd", half, m).tensor_tensor(out=here[:], in0=here[:], in1=gate["f", half, m][:], op=ALU.add)
+            nc.sync.dma_start(out=out[1, m * P:(m + 1) * P, cols], in_=here[:])
+            nc.scalar.activation(out=gate["i", half, m][:], in_=here[:], func=ACT.Tanh)
+
+        def hidden(half, m):
+            cols = slice(half * BANK, (half + 1) * BANK)
+            here = gate["o", half, m]
+            engine_of("hm", half, m).tensor_tensor(out=here[:], in0=here[:], in1=gate["i", half, m][:], op=ALU.mult)
+            nc.sync.dma_start(out=out[0, m * P:(m + 1) * P, cols], in_=here[:])
+
+        banks = BANKS(gate_names)
+        step_of = {}
+        for n in range(len(banks)):
+            step_of[banks[n]] = n
+        due = {}
+        last_step = 0
+        for half in range(HALVES):
+            for m in range(BATCH_TILES):
+                step_fc = step_of["f", half, m] + LAG_PRODUCT
+                step_ic = max(step_of["i", half, m], step_of["c_", half, m]) + LAG_PRODUCT
+                step_c = max(step_fc, step_ic) + LAG_CELL
+                step_h = max(step_of["o", half, m] + LAG_PRODUCT, step_c + LAG_HIDDEN)
+                due.setdefault(step_fc, []).append((2, forget, half, m))
+                due.setdefault(step_ic, []).append((1, remember, half, m))
+                due.setdefault(step_c, []).append((0, cell_state, half, m))
+                due.setdefault(step_h, []).append((3, hidden, half, m))
+                last_step = max(last_step, step_h)
+        for n in range(last_step + 1):
             if n < len(banks):
                 gate_values(*banks[n])
-            if 0 <= n - CELL_LAG < len(banks):
-                cell_state(*banks[n - CELL_LAG])
-            if 0 <= n - PRODUCT_LAG < len(banks):
-                product(*banks[n - PRODUCT_LAG])
+            for rank in range(4):
+                for entry in due.get(n, []):
+                    if entry[0] == rank:
+                        entry[1](entry[2], entry[3])

@@ -27,7 +27,6 @@ WARM_UP = 4
 LAG_PRODUCT = 1
 LAG_CELL = 1
 LAG_HIDDEN = 1
-C_OLD_AFTER = "i"
 
 
 def ON_GPSIMD(op, half, m):
@@ -84,11 +83,11 @@ def tile_create_recurrent_unit_kernel(
         for name in gate_names[1:]:
             nc.vector.memset(planes[name][:].bitcast(I32), 0)
 
-        def load_rows(source, label):
+        def load_rows(source, label, which):
             tiles = []
-            for m in range(BATCH_TILES):
+            for m in which:
                 tiles.append(keep.tile([P, E], BF16, name="%s_%d" % (label, m)))
-                nc.sync.dma_start(out=tiles[m][:], in_=source[m * P:(m + 1) * P, :])
+                nc.sync.dma_start(out=tiles[-1][:], in_=source[m * P:(m + 1) * P, :])
             return tiles
 
         def load_scales(name, s):
@@ -111,19 +110,19 @@ def tile_create_recurrent_unit_kernel(
                     :, :, half * BANK * PACK:(half + 1) * BANK * PACK].bitcast(I32),
             )
 
-        x_rows = load_rows(x, "x_rows")
+        x_rows = load_rows(x, "x_rows", range(BATCH_TILES))
         load_scales("f", 0)
-        h_rows = load_rows(h_prev, "h_rows")
+        h_rows = load_rows(h_prev, "h_rows", range(BATCH_TILES))
         load_scales("f", 1)
         for s in range(SOURCES):
             load_words("f", 0, s)
-        c_old = None
+        c_old = []
         for name in gate_names[1:]:
+            load_scales(name, 0)
             for s in range(SOURCES):
-                load_scales(name, s)
                 load_words(name, 0, s)
-            if name == C_OLD_AFTER:
-                c_old = load_rows(c_prev, "c_old")
+            load_scales(name, 1)
+            c_old.extend(load_rows(c_prev, "c_old", range(len(c_old), min(len(c_old) + 2, BATCH_TILES))))
         for name in gate_names:
             for s in range(SOURCES):
                 load_words(name, 1, s)

@@ -69,7 +69,7 @@ def tile_create_recurrent_unit_kernel(
 
         planes = {}
         for name in gate_names:
-            planes[name] = keep.tile([P, H], U8, align_bytes=64, name="planes_" + name)
+            planes[name] = keep.tile([P, H], U8, align_bytes=256, name="planes_" + name)
         nc.vector.memset(planes[gate_names[0]][:].bitcast(I32), 0)
         ones = keep.tile([P, BANK], BF16, name="ones")
         nc.vector.memset(ones[:], 1.0)
@@ -102,7 +102,7 @@ def tile_create_recurrent_unit_kernel(
         words = {}
 
         def load_words(name, half, s):
-            words[name, half, s] = keep.tile([P, K_GROUPS * BANK * PACK], U8, align_bytes=64,
+            words[name, half, s] = keep.tile([P, K_GROUPS * BANK * PACK], U8, align_bytes=256,
                                              name="words_%s_%d_%d" % (name, half, s))
             nc.sync.dma_start(
                 out=words[name, half, s][:].bitcast(I32).rearrange("p (g w) -> p g w", g=K_GROUPS),
@@ -151,17 +151,17 @@ def tile_create_recurrent_unit_kernel(
                         pairs[:, (K_PASS // 2) * g + u:(K_PASS // 2) * (g + 1):2],
                         identity[:],
                     )
-            grouped = keep.tile([P, K_GROUPS * P * PACK], BF16, align_bytes=64,
+            grouped = keep.tile([P, K_GROUPS * P * PACK], BF16, align_bytes=256,
                                 name="grouped_%d_%d" % (s, m))
             nc.scalar.copy(
                 out=grouped[:].bitcast(F32).rearrange("p (g r u) -> p g r u", g=K_GROUPS, u=2),
                 in_=turned[:].rearrange("p g u r -> p g r u"),
             )
-            codes[s, m] = keep.tile([P, K_GROUPS * P], U32, align_bytes=64, name="codes_%d_%d" % (s, m))
-            code_scales[s, m] = keep.tile([P, K_GROUPS * P], U8, align_bytes=64,
-                                          name="code_scales_%d_%d" % (s, m))
-            nc.vector.quantize_mx(out=codes[s, m][:].bitcast(FP8X4), scales=code_scales[s, m][:],
-                                  in_=grouped[:])
+            for g in range(K_GROUPS):
+                codes[s, m, g] = keep.tile([P, P], U32, align_bytes=256, name="codes_%d_%d_%d" % (s, m, g))
+                code_scales[s, m, g] = keep.tile([P, P], U8, align_bytes=256, name="code_scales_%d_%d_%d" % (s, m, g))
+                nc.vector.quantize_mx(out=codes[s, m, g][:].bitcast(FP8X4), scales=code_scales[s, m, g][:],
+                                      in_=grouped[:, g * P * PACK:(g + 1) * P * PACK])
 
         unread = psum.tile([P, BANK], F32, tag="bank", name="unread")
         for repeat in range(WARM_UP):
@@ -182,8 +182,8 @@ def tile_create_recurrent_unit_kernel(
                     top = SCALE_ROWS * (K_GROUPS * s + g)
                     nc.tensor.matmul_mx(
                         out=acc[:],
-                        lhsT=codes[s, m][:, g * P:(g + 1) * P].bitcast(FP8X4),
-                        lhsT_scale=code_scales[s, m][:, g * P:(g + 1) * P],
+                        lhsT=codes[s, m, g][:].bitcast(FP8X4),
+                        lhsT_scale=code_scales[s, m, g][:],
                         rhs=words[name, half, s][:, g * BANK * PACK:(g + 1) * BANK * PACK].bitcast(FP8X4),
                         rhs_scale=planes[name][top:P, cols],
                         start=(s == 0 and g == 0),

@@ -135,8 +135,8 @@ def tile_create_recurrent_unit_kernel(
                 cols = slice(half * BANK, (half + 1) * BANK)
                 nc.tensor.matmul(out=spread[:, cols], lhsT=ones[:, :P], rhs=bias_row[name][:, cols],
                                  start=True, stop=True)
-            bias_all[name] = keep.tile([P, H], BF16, name="bias_all_" + name)
-            nc.vector.tensor_copy(out=bias_all[name][:], in_=spread[:])
+            bias_all[name] = keep.tile([P, H], BF16, align_bytes=256, name="bias_all_" + name)
+            nc.scalar.copy(out=bias_all[name][:], in_=spread[:])
 
         codes = {}
         code_scales = {}
@@ -168,11 +168,19 @@ def tile_create_recurrent_unit_kernel(
             nc.tensor.matmul(out=unread[:], lhsT=ones[:, :P], rhs=ones[:], start=True, stop=True)
         for m in range(BATCH_TILES):
             quantise_rows(0, m, x_rows[m][:])
+        spread_bias(gate_names[0])
         for m in range(BATCH_TILES):
             quantise_rows(1, m, h_rows[m][:])
-            spread_bias(gate_names[m])
+            if m == BATCH_TILES // 2 - 1:
+                spread_bias(gate_names[1])
+        for name in gate_names[2:]:
+            spread_bias(name)
 
         gate = {}
+
+        def pieces(name, half, m):
+            count = 2 if (name, half, m) == ("o", HALVES - 1, BATCH_TILES - 1) else 1
+            return [slice(k * BANK // count, (k + 1) * BANK // count) for k in range(count)]
 
         def gate_values(name, half, m):
             cols = slice(half * BANK, (half + 1) * BANK)
@@ -189,11 +197,13 @@ def tile_create_recurrent_unit_kernel(
                         start=(s == 0 and g == 0),
                         stop=(s == SOURCES - 1 and g == K_GROUPS - 1),
                     )
-            gate[name, half, m] = keep.tile([P, BANK], F32, name="gate_%s_%d_%d" % (name, half, m))
-            nc.vector.tensor_tensor(out=gate[name, half, m][:], in0=acc[:],
-                                    in1=bias_all[name][:, cols], op=ALU.add)
-            nc.scalar.activation(out=gate[name, half, m][:], in_=gate[name, half, m][:],
-                                 func=gate_func[name])
+            here = keep.tile([P, BANK], F32, align_bytes=256, name="gate_%s_%d_%d" % (name, half, m))
+            gate[name, half, m] = here
+            for part in pieces(name, half, m):
+                bias_part = slice(half * BANK + part.start, half * BANK + part.stop)
+                nc.vector.tensor_tensor(out=here[:, part], in0=acc[:, part],
+                                        in1=bias_all[name][:, bias_part], op=ALU.add)
+                nc.scalar.activation(out=here[:, part], in_=here[:, part], func=gate_func[name])
 
         def engine_of(op, half, m):
             return nc.gpsimd if ON_GPSIMD(op, half, m) else nc.vector
@@ -215,10 +225,12 @@ def tile_create_recurrent_unit_kernel(
             nc.scalar.activation(out=gate["i", half, m][:], in_=here[:], func=ACT.Tanh)
 
         def hidden(half, m):
-            cols = slice(half * BANK, (half + 1) * BANK)
             here = gate["o", half, m]
-            engine_of("hm", half, m).tensor_tensor(out=here[:], in0=here[:], in1=gate["i", half, m][:], op=ALU.mult)
-            nc.sync.dma_start(out=out[0, m * P:(m + 1) * P, cols], in_=here[:])
+            for part in pieces("o", half, m):
+                engine_of("hm", half, m).tensor_tensor(out=here[:, part], in0=here[:, part],
+                                                       in1=gate["i", half, m][:, part], op=ALU.mult)
+                nc.sync.dma_start(out=out[0, m * P:(m + 1) * P, half * BANK + part.start:half * BANK + part.stop],
+                                  in_=here[:, part])
 
         banks = BANKS(gate_names)
         step_of = {}

@@ -20,6 +20,7 @@ K_GROUPS = E // K_PASS
 BANK = 512
 BATCH_TILES = BATCH // P
 HALVES = H // BANK
+CHUNKS = BANK // P
 SOURCES = 2
 QUADRANTS = 4
 SCALE_ROWS = 4
@@ -35,7 +36,7 @@ def ON_GPSIMD(op, half, m):
 
 def BANKS(gate_names):
     return ([(name, 0, m) for name in gate_names for m in range(BATCH_TILES)]
-            + [(name, 1, 2 * pair + e) for pair in range(2) for name in gate_names for e in range(2)])
+            + [(name, 1, 2 * pair + e) for pair in range(2) for name in gate_names for e in range(2)])[:-2]
 
 
 FLOPS = 2 * BATCH * (E + H) * 4 * H
@@ -158,9 +159,13 @@ def tile_create_recurrent_unit_kernel(
                 in_=turned[:].rearrange("p g u r -> p g r u"),
             )
             for g in range(K_GROUPS):
-                codes[s, m, g] = keep.tile([P, P], U32, align_bytes=256, name="codes_%d_%d_%d" % (s, m, g))
-                code_scales[s, m, g] = keep.tile([P, P], U8, align_bytes=256, name="code_scales_%d_%d_%d" % (s, m, g))
-                nc.vector.quantize_mx(out=codes[s, m, g][:].bitcast(FP8X4), scales=code_scales[s, m, g][:],
+                if m % 2 == 0:
+                    codes[s, m // 2, g] = keep.tile([P, 2 * P], U32, align_bytes=256, name="codes_%d_%d_%d" % (s, m, g))
+                    code_scales[s, m // 2, g] = keep.tile([P, 2 * P], U8, align_bytes=256,
+                                                          name="code_scales_%d_%d_%d" % (s, m, g))
+                rows = slice(m % 2 * P, (m % 2 + 1) * P)
+                nc.vector.quantize_mx(out=codes[s, m // 2, g][:, rows].bitcast(FP8X4),
+                                      scales=code_scales[s, m // 2, g][:, rows],
                                       in_=grouped[:, g * P * PACK:(g + 1) * P * PACK])
 
         unread = psum.tile([P, BANK], F32, tag="bank", name="unread")
@@ -175,6 +180,13 @@ def tile_create_recurrent_unit_kernel(
                 spread_bias(gate_names[1])
         for name in gate_names[2:]:
             spread_bias(name)
+        columns = psum.tile([P, 2 * CHUNKS], F32, tag="bank", name="columns")
+        for chunk in range(CHUNKS):
+            first = (HALVES - 1) * BANK + chunk * P
+            nc.tensor.matmul(out=columns[:, 2 * chunk:2 * chunk + 2], lhsT=bias_row["o"][:, first:first + P],
+                             rhs=ones[:, 0:2], start=True, stop=True)
+        bias_columns = keep.tile([P, 2 * CHUNKS], F32, name="bias_columns")
+        nc.scalar.copy(out=bias_columns[:], in_=columns[:])
 
         gate = {}
 
@@ -182,16 +194,51 @@ def tile_create_recurrent_unit_kernel(
             count = 2 if (name, half, m) == ("o", HALVES - 1, BATCH_TILES - 1) else 1
             return [slice(k * BANK // count, (k + 1) * BANK // count) for k in range(count)]
 
+        turned_o = {}
+
+        def last_o(chunk):
+            first = (HALVES - 1) * BANK + chunk * P
+            acc = psum.tile([P, 2 * P], F32, tag="bank", name="acc_last_o_%d" % chunk)
+            for s in range(SOURCES):
+                for g in range(K_GROUPS):
+                    top = SCALE_ROWS * (K_GROUPS * s + g)
+                    word = g * BANK + chunk * P
+                    nc.tensor.matmul_mx(
+                        out=acc[:],
+                        lhsT=words["o", HALVES - 1, s][:, word * PACK:(word + P) * PACK].bitcast(FP8X4),
+                        lhsT_scale=planes["o"][top:P, first:first + P],
+                        rhs=codes[s, 1, g][:].bitcast(FP8X4),
+                        rhs_scale=code_scales[s, 1, g][:],
+                        start=(s == 0 and g == 0),
+                        stop=(s == SOURCES - 1 and g == K_GROUPS - 1),
+                    )
+            turned_o[chunk] = keep.tile([P, 2 * P], F32, align_bytes=256, name="turned_o_%d" % chunk)
+            nc.scalar.activation(out=turned_o[chunk][:], in_=acc[:], func=ACT.Sigmoid,
+                                 bias=bias_columns[:, 2 * chunk:2 * chunk + 1])
+
+        def last_hidden(m):
+            back = psum.tile([P, BANK], F32, tag="bank", name="back_%d" % m)
+            for chunk in range(CHUNKS):
+                nc.tensor.transpose(back[:, chunk * P:(chunk + 1) * P], turned_o[chunk][:, m % 2 * P:(m % 2 + 1) * P],
+                                    identity[:])
+            here = keep.tile([P, BANK], F32, align_bytes=256, name="last_h_%d" % m)
+            half = HALVES - 1
+            for part in pieces("o", half, m):
+                nc.vector.tensor_tensor(out=here[:, part], in0=back[:, part], in1=gate["i", half, m][:, part], op=ALU.mult)
+                nc.sync.dma_start(out=out[0, m * P:(m + 1) * P, half * BANK + part.start:half * BANK + part.stop],
+                                  in_=here[:, part])
+
         def gate_values(name, half, m):
             cols = slice(half * BANK, (half + 1) * BANK)
+            rows = slice(m % 2 * P, (m % 2 + 1) * P)
             acc = psum.tile([P, BANK], F32, tag="bank", name="acc_%s_%d_%d" % (name, half, m))
             for s in range(SOURCES):
                 for g in range(K_GROUPS):
                     top = SCALE_ROWS * (K_GROUPS * s + g)
                     nc.tensor.matmul_mx(
                         out=acc[:],
-                        lhsT=codes[s, m, g][:].bitcast(FP8X4),
-                        lhsT_scale=code_scales[s, m, g][:],
+                        lhsT=codes[s, m // 2, g][:, rows].bitcast(FP8X4),
+                        lhsT_scale=code_scales[s, m // 2, g][:, rows],
                         rhs=words[name, half, s][:, g * BANK * PACK:(g + 1) * BANK * PACK].bitcast(FP8X4),
                         rhs_scale=planes[name][top:P, cols],
                         start=(s == 0 and g == 0),
@@ -243,16 +290,24 @@ def tile_create_recurrent_unit_kernel(
                 step_fc = step_of["f", half, m] + LAG_PRODUCT
                 step_ic = max(step_of["i", half, m], step_of["c_", half, m]) + LAG_PRODUCT
                 step_c = max(step_fc, step_ic) + LAG_CELL
-                step_h = max(step_of["o", half, m] + LAG_PRODUCT, step_c + LAG_HIDDEN)
+                if half == HALVES - 1:
+                    step_c = max(step_c, step_of["c_", half, m - m % 2 + 1] + LAG_PRODUCT + LAG_CELL)
+                step_h = max(step_of.get(("o", half, m), 0) + LAG_PRODUCT, step_c + LAG_HIDDEN)
                 due.setdefault(step_fc, []).append((2, forget, half, m))
                 due.setdefault(step_ic, []).append((1, remember, half, m))
                 due.setdefault(step_c, []).append((0, cell_state, half, m))
-                due.setdefault(step_h, []).append((3, hidden, half, m))
+                if ("o", half, m) in step_of:
+                    due.setdefault(step_h, []).append((3, hidden, half, m))
                 last_step = max(last_step, step_h)
         for n in range(last_step + 1):
             if n < len(banks):
                 gate_values(*banks[n])
+            elif n == len(banks):
+                for chunk in range(CHUNKS):
+                    last_o(chunk)
             for rank in range(4):
                 for entry in due.get(n, []):
                     if entry[0] == rank:
                         entry[1](entry[2], entry[3])
+        for m in (BATCH_TILES - 2, BATCH_TILES - 1):
+            last_hidden(m)

@@ -190,8 +190,8 @@ def tile_create_recurrent_unit_kernel(
 
         gate = {}
 
-        def pieces(name, half, m):
-            count = 2 if (name, half, m) == ("o", HALVES - 1, BATCH_TILES - 1) else 1
+        def pieces(half, m):
+            count = 2 if half == HALVES - 1 and m >= BATCH_TILES - 2 else 1
             return [slice(k * BANK // count, (k + 1) * BANK // count) for k in range(count)]
 
         turned_o = {}
@@ -223,7 +223,7 @@ def tile_create_recurrent_unit_kernel(
                                     identity[:])
             here = keep.tile([P, BANK], F32, align_bytes=256, name="last_h_%d" % m)
             half = HALVES - 1
-            for part in pieces("o", half, m):
+            for part in pieces(half, m):
                 nc.vector.tensor_tensor(out=here[:, part], in0=back[:, part], in1=gate["i", half, m][:, part], op=ALU.mult)
                 nc.sync.dma_start(out=out[0, m * P:(m + 1) * P, half * BANK + part.start:half * BANK + part.stop],
                                   in_=here[:, part])
@@ -246,11 +246,8 @@ def tile_create_recurrent_unit_kernel(
                     )
             here = keep.tile([P, BANK], F32, align_bytes=256, name="gate_%s_%d_%d" % (name, half, m))
             gate[name, half, m] = here
-            for part in pieces(name, half, m):
-                bias_part = slice(half * BANK + part.start, half * BANK + part.stop)
-                nc.vector.tensor_tensor(out=here[:, part], in0=acc[:, part],
-                                        in1=bias_all[name][:, bias_part], op=ALU.add)
-                nc.scalar.activation(out=here[:, part], in_=here[:, part], func=gate_func[name])
+            nc.vector.tensor_tensor(out=here[:], in0=acc[:], in1=bias_all[name][:, cols], op=ALU.add)
+            nc.scalar.activation(out=here[:], in_=here[:], func=gate_func[name])
 
         def engine_of(op, half, m):
             return nc.gpsimd if ON_GPSIMD(op, half, m) else nc.vector
@@ -269,15 +266,14 @@ def tile_create_recurrent_unit_kernel(
             here = gate["c_", half, m]
             engine_of("cadd", half, m).tensor_tensor(out=here[:], in0=here[:], in1=gate["f", half, m][:], op=ALU.add)
             nc.sync.dma_start(out=out[1, m * P:(m + 1) * P, cols], in_=here[:])
-            nc.scalar.activation(out=gate["i", half, m][:], in_=here[:], func=ACT.Tanh)
+            for part in pieces(half, m):
+                nc.scalar.activation(out=gate["i", half, m][:, part], in_=here[:, part], func=ACT.Tanh)
 
         def hidden(half, m):
+            cols = slice(half * BANK, (half + 1) * BANK)
             here = gate["o", half, m]
-            for part in pieces("o", half, m):
-                engine_of("hm", half, m).tensor_tensor(out=here[:, part], in0=here[:, part],
-                                                       in1=gate["i", half, m][:, part], op=ALU.mult)
-                nc.sync.dma_start(out=out[0, m * P:(m + 1) * P, half * BANK + part.start:half * BANK + part.stop],
-                                  in_=here[:, part])
+            engine_of("hm", half, m).tensor_tensor(out=here[:], in0=here[:], in1=gate["i", half, m][:], op=ALU.mult)
+            nc.sync.dma_start(out=out[0, m * P:(m + 1) * P, cols], in_=here[:])
 
         banks = BANKS(gate_names)
         step_of = {}

from contextlib import ExitStack

import concourse.mybir as mybir
from concourse.masks import make_identity

F32 = mybir.dt.float32
BF16 = mybir.dt.bfloat16
I32 = mybir.dt.int32
U32 = mybir.dt.uint32
U8 = mybir.dt.uint8
FP8X4 = mybir.dt.float8_e4m3fn_x4
ACT = mybir.ActivationFunctionType
ALU = mybir.AluOpType

P = 128
BATCH, E, H = 512, 1024, 1024
PACK = 4
K_PASS = P * PACK
K_GROUPS = E // K_PASS
BANK = 512
BATCH_TILES = BATCH // P
HALVES = H // BANK
CHUNKS = BANK // P
SOURCES = 2
QUADRANTS = 4
SCALE_ROWS = 4
WARM_UP = 4
LAG_PRODUCT = 1
LAG_CELL = 1
LAG_HIDDEN = 1


def ON_GPSIMD(op, half, m):
    return op == "fc"


def BANKS(gate_names):
    return ([(name, 0, m) for name in gate_names for m in range(BATCH_TILES)]
            + [(name, 1, 2 * pair + e) for pair in range(2) for name in gate_names for e in range(2)])[:-2]


FLOPS = 2 * BATCH * (E + H) * 4 * H


def tile_create_recurrent_unit_kernel(
    tc,
    x, hidden_memory_tm1,
    Wi_words, Wi_scales, Ui_words, Ui_scales, bi,
    Wf_words, Wf_scales, Uf_words, Uf_scales, bf,
    Wog_words, Wog_scales, Uog_words, Uog_scales, bog,
    Wc_words, Wc_scales, Uc_words, Uc_scales, bc,
    out,
):
    nc = tc.nc
    h_prev = hidden_memory_tm1[0]
    c_prev = hidden_memory_tm1[1]

    gate_names = ["f", "i", "c_", "o"]
    gate_words = {"i": (Wi_words, Ui_words), "c_": (Wc_words, Uc_words),
                  "f": (Wf_words, Uf_words), "o": (Wog_words, Uog_words)}
    gate_scales = {"i": (Wi_scales, Ui_scales), "c_": (Wc_scales, Uc_scales),
                   "f": (Wf_scales, Uf_scales), "o": (Wog_scales, Uog_scales)}
    gate_bias = {"i": bi, "c_": bc, "f": bf, "o": bog}
    gate_func = {"i": ACT.Sigmoid, "c_": ACT.Tanh, "f": ACT.Sigmoid, "o": ACT.Sigmoid}

    with ExitStack() as ctx:
        keep = ctx.enter_context(tc.tile_pool(name="keep", bufs=1))
        psum = ctx.enter_context(tc.psum_pool(name="psum", bufs=8))
        ctx.enter_context(tc.manual_schedule())

        planes = {}
        for name in gate_names:
            planes[name] = keep.tile([P, H], U8, align_bytes=256, name="planes_" + name)
        nc.vector.memset(planes[gate_names[0]][:].bitcast(I32), 0)
        ones = keep.tile([P, BANK], BF16, name="ones")
        nc.vector.memset(ones[:], 1.0)
        identity = keep.tile([P, P], F32, name="identity")
        make_identity(nc, identity[:])
        bias_row = {}
        for name in gate_names:
            bias_row[name] = keep.tile([P, H], BF16, name="bias_row_" + name)
            nc.vector.memset(bias_row[name][:].bitcast(I32), 0)
            nc.gpsimd.dma_start(out=bias_row[name][0:1, :], in_=gate_bias[name].unsqueeze(0))
        for name in gate_names[1:]:
            nc.vector.memset(planes[name][:].bitcast(I32), 0)

        def load_rows(source, label, which):
            tiles = []
            for m in which:
                tiles.append(keep.tile([P, E], BF16, name="%s_%d" % (label, m)))
                nc.sync.dma_start(out=tiles[-1][:], in_=source[m * P:(m + 1) * P, :])
            return tiles

        def load_scales(name, s):
            for quadrant in range(QUADRANTS):
                top = 32 * quadrant + SCALE_ROWS * K_GROUPS * s
                nc.sync.dma_start(
                    out=planes[name][top:top + SCALE_ROWS * K_GROUPS, :].bitcast(I32),
                    in_=gate_scales[name][s][
                        :, SCALE_ROWS * quadrant:SCALE_ROWS * (quadrant + 1), :].bitcast(I32),
                )

        words = {}

        def load_words(name, half, s):
            words[name, half, s] = keep.tile([P, K_GROUPS * BANK * PACK], U8, align_bytes=256,
                                             name="words_%s_%d_%d" % (name, half, s))
            nc.sync.dma_start(
                out=words[name, half, s][:].bitcast(I32).rearrange("p (g w) -> p g w", g=K_GROUPS),
                in_=gate_words[name][s].rearrange("g p n t -> p g (n t)")[
                    :, :, half * BANK * PACK:(half + 1) * BANK * PACK].bitcast(I32),
            )

        x_rows = load_rows(x, "x_rows", range(BATCH_TILES))
        load_scales("f", 0)
        h_rows = load_rows(h_prev, "h_rows", range(BATCH_TILES))
        load_scales("f", 1)
        for s in range(SOURCES):
            load_words("f", 0, s)
        c_old = []
        for name in gate_names[1:]:
            load_scales(name, 0)
            for s in range(SOURCES):
                load_words(name, 0, s)
            load_scales(name, 1)
            c_old.extend(load_rows(c_prev, "c_old", range(len(c_old), min(len(c_old) + 2, BATCH_TILES))))
        for name in gate_names:
            for s in range(SOURCES):
                load_words(name, 1, s)

        bias_all = {}

        def spread_bias(name):
            spread = psum.tile([P, H], BF16, tag="bank", name="spread_" + name)
            for half in range(HALVES):
                cols = slice(half * BANK, (half + 1) * BANK)
                nc.tensor.matmul(out=spread[:, cols], lhsT=ones[:, :P], rhs=bias_row[name][:, cols],
                                 start=True, stop=True)
            bias_all[name] = keep.tile([P, H], BF16, align_bytes=256, name="bias_all_" + name)
            nc.scalar.copy(out=bias_all[name][:], in_=spread[:])

        codes = {}
        code_scales = {}

        def quantise_rows(s, m, bf16_rows):
            pairs = bf16_rows.bitcast(F32)
            turned = psum.tile([P, K_GROUPS, 2, P], F32, tag="bank", name="turned_%d_%d" % (s, m))
            for g in range(K_GROUPS):
                for u in range(2):
                    nc.tensor.transpose(
                        turned[:, g, u, :],
                        pairs[:, (K_PASS // 2) * g + u:(K_PASS // 2) * (g + 1):2],
                        identity[:],
                    )
            grouped = keep.tile([P, K_GROUPS * P * PACK], BF16, align_bytes=256,
                                name="grouped_%d_%d" % (s, m))
            nc.scalar.copy(
                out=grouped[:].bitcast(F32).rearrange("p (g r u) -> p g r u", g=K_GROUPS, u=2),
                in_=turned[:].rearrange("p g u r -> p g r u"),
            )
            for g in range(K_GROUPS):
                if m % 2 == 0:
                    codes[s, m // 2, g] = keep.tile([P, 2 * P], U32, align_bytes=256, name="codes_%d_%d_%d" % (s, m, g))
                    code_scales[s, m // 2, g] = keep.tile([P, 2 * P], U8, align_bytes=256,
                                                          name="code_scales_%d_%d_%d" % (s, m, g))
                rows = slice(m % 2 * P, (m % 2 + 1) * P)
                nc.vector.quantize_mx(out=codes[s, m // 2, g][:, rows].bitcast(FP8X4),
                                      scales=code_scales[s, m // 2, g][:, rows],
                                      in_=grouped[:, g * P * PACK:(g + 1) * P * PACK])

        unread = psum.tile([P, BANK], F32, tag="bank", name="unread")
        for repeat in range(WARM_UP):
            nc.tensor.matmul(out=unread[:], lhsT=ones[:, :P], rhs=ones[:], start=True, stop=True)
        for m in range(BATCH_TILES):
            quantise_rows(0, m, x_rows[m][:])
        spread_bias(gate_names[0])
        for m in range(BATCH_TILES):
            quantise_rows(1, m, h_rows[m][:])
            if m == BATCH_TILES // 2 - 1:
                spread_bias(gate_names[1])
        for name in gate_names[2:]:
            spread_bias(name)
        columns = psum.tile([P, 2 * CHUNKS], F32, tag="bank", name="columns")
        for chunk in range(CHUNKS):
            first = (HALVES - 1) * BANK + chunk * P
            nc.tensor.matmul(out=columns[:, 2 * chunk:2 * chunk + 2], lhsT=bias_row["o"][:, first:first + P],
                             rhs=ones[:, 0:2], start=True, stop=True)
        bias_columns = keep.tile([P, 2 * CHUNKS], F32, name="bias_columns")
        nc.scalar.copy(out=bias_columns[:], in_=columns[:])

        gate = {}

        def pieces(half, m):
            count = 2 if half == HALVES - 1 and m >= BATCH_TILES - 2 else 1
            return [slice(k * BANK // count, (k + 1) * BANK // count) for k in range(count)]

        turned_o = {}

        def last_o(chunk):
            first = (HALVES - 1) * BANK + chunk * P
            acc = psum.tile([P, 2 * P], F32, tag="bank", name="acc_last_o_%d" % chunk)
            for s in range(SOURCES):
                for g in range(K_GROUPS):
                    top = SCALE_ROWS * (K_GROUPS * s + g)
                    word = g * BANK + chunk * P
                    nc.tensor.matmul_mx(
                        out=acc[:],
                        lhsT=words["o", HALVES - 1, s][:, word * PACK:(word + P) * PACK].bitcast(FP8X4),
                        lhsT_scale=planes["o"][top:P, first:first + P],
                        rhs=codes[s, 1, g][:].bitcast(FP8X4),
                        rhs_scale=code_scales[s, 1, g][:],
                        start=(s == 0 and g == 0),
                        stop=(s == SOURCES - 1 and g == K_GROUPS - 1),
                    )
            turned_o[chunk] = keep.tile([P, 2 * P], F32, align_bytes=256, name="turned_o_%d" % chunk)
            nc.scalar.activation(out=turned_o[chunk][:], in_=acc[:], func=ACT.Sigmoid,
                                 bias=bias_columns[:, 2 * chunk:2 * chunk + 1])

        def last_hidden(m):
            back = psum.tile([P, BANK], F32, tag="bank", name="back_%d" % m)
            for chunk in range(CHUNKS):
                nc.tensor.transpose(back[:, chunk * P:(chunk + 1) * P], turned_o[chunk][:, m % 2 * P:(m % 2 + 1) * P],
                                    identity[:])
            here = keep.tile([P, BANK], F32, align_bytes=256, name="last_h_%d" % m)
            half = HALVES - 1
            for part in pieces(half, m):
                nc.vector.tensor_tensor(out=here[:, part], in0=back[:, part], in1=gate["i", half, m][:, part], op=ALU.mult)
                nc.sync.dma_start(out=out[0, m * P:(m + 1) * P, half * BANK + part.start:half * BANK + part.stop],
                                  in_=here[:, part])

        def gate_values(name, half, m):
            cols = slice(half * BANK, (half + 1) * BANK)
            rows = slice(m % 2 * P, (m % 2 + 1) * P)
            acc = psum.tile([P, BANK], F32, tag="bank", name="acc_%s_%d_%d" % (name, half, m))
            for s in range(SOURCES):
                for g in range(K_GROUPS):
                    top = SCALE_ROWS * (K_GROUPS * s + g)
                    nc.tensor.matmul_mx(
                        out=acc[:],
                        lhsT=codes[s, m // 2, g][:, rows].bitcast(FP8X4),
                        lhsT_scale=code_scales[s, m // 2, g][:, rows],
                        rhs=words[name, half, s][:, g * BANK * PACK:(g + 1) * BANK * PACK].bitcast(FP8X4),
                        rhs_scale=planes[name][top:P, cols],
                        start=(s == 0 and g == 0),
                        stop=(s == SOURCES - 1 and g == K_GROUPS - 1),
                    )
            here = keep.tile([P, BANK], F32, align_bytes=256, name="gate_%s_%d_%d" % (name, half, m))
            gate[name, half, m] = here
            nc.vector.tensor_tensor(out=here[:], in0=acc[:], in1=bias_all[name][:, cols], op=ALU.add)
            nc.scalar.activation(out=here[:], in_=here[:], func=gate_func[name])

        def engine_of(op, half, m):
            return nc.gpsimd if ON_GPSIMD(op, half, m) else nc.vector

        def forget(half, m):
            cols = slice(half * BANK, (half + 1) * BANK)
            here = gate["f", half, m]
            engine_of("fc", half, m).tensor_tensor(out=here[:], in0=here[:], in1=c_old[m][:, cols], op=ALU.mult)

        def remember(half, m):
            here = gate["c_", half, m]
            engine_of("ic", half, m).tensor_tensor(out=here[:], in0=here[:], in1=gate["i", half, m][:], op=ALU.mult)

        def cell_state(half, m):
            cols = slice(half * BANK, (half + 1) * BANK)
            here = gate["c_", half, m]
            engine_of("cadd", half, m).tensor_tensor(out=here[:], in0=here[:], in1=gate["f", half, m][:], op=ALU.add)
            nc.sync.dma_start(out=out[1, m * P:(m + 1) * P, cols], in_=here[:])
            for part in pieces(half, m):
                nc.scalar.activation(out=gate["i", half, m][:, part], in_=here[:, part], func=ACT.Tanh)

        def hidden(half, m):
            cols = slice(half * BANK, (half + 1) * BANK)
            here = gate["o", half, m]
            engine_of("hm", half, m).tensor_tensor(out=here[:], in0=here[:], in1=gate["i", half, m][:], op=ALU.mult)
            nc.sync.dma_start(out=out[0, m * P:(m + 1) * P, cols], in_=here[:])

        banks = BANKS(gate_names)
        step_of = {}
        for n in range(len(banks)):
            step_of[banks[n]] = n
        due = {}
        last_step = 0
        for half in range(HALVES):
            for m in range(BATCH_TILES):
                step_fc = step_of["f", half, m] + LAG_PRODUCT
                step_ic = max(step_of["i", half, m], step_of["c_", half, m]) + LAG_PRODUCT
                step_c = max(step_fc, step_ic) + LAG_CELL
                if half == HALVES - 1:
                    step_c = max(step_c, step_of["c_", half, m - m % 2 + 1] + LAG_PRODUCT + LAG_CELL)
                step_h = max(step_of.get(("o", half, m), 0) + LAG_PRODUCT, step_c + LAG_HIDDEN)
                due.setdefault(step_fc, []).append((2, forget, half, m))
                due.setdefault(step_ic, []).append((1, remember, half, m))
                due.setdefault(step_c, []).append((0, cell_state, half, m))
                if ("o", half, m) in step_of:
                    due.setdefault(step_h, []).append((3, hidden, half, m))
                last_step = max(last_step, step_h)
        for n in range(last_step + 1):
            if n < len(banks):
                gate_values(*banks[n])
            elif n == len(banks):
                for chunk in range(CHUNKS):
                    last_o(chunk)
            for rank in range(4):
                for entry in due.get(n, []):
                    if entry[0] == rank:
                        entry[1](entry[2], entry[3])
        for m in (BATCH_TILES - 2, BATCH_TILES - 1):
            last_hidden(m)
